import numpy as np
import ml_dtypes


def mxq(x, axis, fmt="e4m3"):
    dtype, down = {"e4m3": (ml_dtypes.float8_e4m3fn, 7), "e5m2": (ml_dtypes.float8_e5m2, 14)}[fmt]
    v = np.moveaxis(np.asarray(x, np.float32).astype(ml_dtypes.bfloat16).astype(np.float64), axis, -1)
    blocks = v.reshape(v.shape[:-1] + (-1, 32))
    amax = np.abs(blocks).max(-1, keepdims=True)
    byte = np.maximum(np.where(amax > 0, np.frexp(amax)[1] - 1 + 127, 0) - down, 1)
    scale = np.exp2(byte - 127.0)
    codes = (blocks / scale).astype(np.float32).astype(dtype).astype(np.float64)
    return np.moveaxis((codes * scale).reshape(v.shape), -1, axis)


WIDE = False


def mx_kscale(k):
    if not WIDE:
        return np.ones(k)
    levels = np.array([10, -10, 5, -5, 0])
    if k % 512:
        return np.exp2(np.random.permutation(np.resize(levels, k // 32))).repeat(32)
    a = np.empty((k // 512, 16))
    for p in range(k // 512):
        a[p, :8] = np.random.permutation(np.resize(levels, 8))
        for g in range(8):
            far = levels[np.abs(levels - a[p, g]) >= 10]
            a[p, g + 8] = far[np.random.randint(len(far))]
    return np.exp2(a.ravel()).repeat(32)


BF16 = ml_dtypes.bfloat16


def bf(x):
    return np.asarray(x, np.float32).astype(BF16)


def f64(x):
    return np.asarray(x).astype(np.float64)


L, D, HQ, HKV, HD, WIN, ROPE_BASE = 512, 2048, 16, 4, 128, 256, 1024
HALF = HD // 2
QUART = HALF // 2
NQ = HQ * HD
NKV = HKV * HD


def rope_tables():
    freqs = (1.0 / ROPE_BASE) ** np.linspace(0.0, 1.0, num=QUART)
    freqs = np.concatenate([freqs, np.zeros(QUART)])
    theta = np.arange(L, dtype=np.float64)[:, None] * freqs[None, :]
    return np.cos(theta)[:, None, :], np.sin(theta)[:, None, :]


def rotate(u, cos, sin):
    u1, u2 = u[..., :HALF], u[..., HALF:]
    return np.concatenate([u1 * cos + u2 * sin, -u1 * sin + u2 * cos], axis=-1)


def draw0():
    s = mx_kscale(D)
    return {"x": bf(np.random.standard_normal((L, D)) * s),
            "Wqkv": bf(np.random.standard_normal((D, NQ + NKV + NKV)) * 1.25 / np.sqrt(D) / s[:, None])}


def core(x, Wqkv):
    proj = mxq(f64(x), 1, "e4m3") @ mxq(f64(Wqkv), 0, "e4m3")
    q = proj[:, :NQ].reshape(L, HQ, HD)
    k = proj[:, NQ:NQ + NKV].reshape(L, HKV, HD)
    v = proj[:, NQ + NKV:].reshape(L, HKV, HD)
    cos, sin = rope_tables()
    return rotate(q, cos, sin), rotate(k, cos, sin), v


def e4m3fn_bytes(y):
    return np.clip(np.asarray(y, np.float64), -448.0, 448.0).astype(np.float32).astype(ml_dtypes.float8_e4m3fn).view(np.uint8)


def e4m3fn_values(b):
    return np.asarray(b, np.uint8).view(ml_dtypes.float8_e4m3fn).astype(np.float64)


def setup_inputs():
    d = draw0()
    x0 = np.asarray(d['Wqkv']).astype(np.float64)
    s = (np.max(np.abs(x0), axis=(1,), keepdims=True) / 448.0).astype(np.float32)
    out = {}
    for k, v in d.items():
        if k == 'Wqkv':
            out['Wqkv_bytes'] = e4m3fn_bytes(x0 / s.astype(np.float64))
            out['Wqkv_scale'] = s
        else:
            out[k] = v
    return out


def reference(x, Wqkv_bytes, Wqkv_scale):
    return core(x, e4m3fn_values(Wqkv_bytes) * Wqkv_scale.astype(np.float64))

@@ -1,0 +1,361 @@
+import math
+from contextlib import ExitStack
+
+import concourse.mybir as mybir
+from concourse.masks import make_identity
+
+FLOPS = 2 * 512 * 2048 * 3072
+
+F32 = mybir.dt.float32
+BF16 = mybir.dt.bfloat16
+I32 = mybir.dt.int32
+U32 = mybir.dt.uint32
+U8 = mybir.dt.uint8
+FP8 = mybir.dt.float8_e4m3fn
+FP8X4 = mybir.dt.float8_e4m3fn_x4
+ALU = mybir.AluOpType
+ACT = mybir.ActivationFunctionType
+
+P = 128
+PACK = 4
+PASSES = 4
+MT = 4
+ROT = 32
+RUN = 4
+
+UNITS = (("q", 0, 1024), ("q", 1024, 1024), ("k", 2048, 512), ("v", 2560, 512))
+
+V_WIDEN = {(0, 0), (0, 1), (0, 2), (0, 3), (1, 2), (1, 3), (2, 3), (3, 3)}
+S_INTER = (15,)
+HEAD_PLANES = ((1, 0), (0, 0), (0, 1), (1, 1), (0, 2), (0, 3), (1, 2), (1, 3))
+G_SUMS = (0, 1)
+X_EVAC_ON_S = (0, 1, 2, 3, 4, 5, 6, 7)
+
+
+def rope_angles(nc, const):
+    pos_i = const.tile([P, MT], I32, name="pos_i")
+    nc.gpsimd.iota(pos_i[:], pattern=[[P, MT]], base=0, channel_multiplier=1)
+    freq = const.tile([P, ROT], F32, name="freq")
+    nc.vector.memset(freq[:], 1.0)
+    pos = const.tile([P, MT], F32, name="pos")
+    nc.vector.tensor_copy(out=pos[:], in_=pos_i[:])
+    for w in (1, 4, 16):
+        for r in range(1, min(4, ROT // w)):
+            nc.vector.tensor_scalar(
+                out=freq[:, r * w : (r + 1) * w],
+                in0=freq[:, 0:w],
+                scalar1=(1.0 / 1024.0) ** (r * w / 31.0),
+                scalar2=None,
+                op0=ALU.mult,
+            )
+    ang = const.tile([P, 2, MT, ROT], F32, name="ang")
+    for m in range(MT):
+        nc.vector.tensor_scalar(out=ang[:, 0, m, :], in0=freq[:], scalar1=pos[:, m : m + 1], scalar2=None, op0=ALU.mult)
+        nc.vector.tensor_scalar(
+            out=ang[:, 1, m, :], in0=freq[:], scalar1=pos[:, m : m + 1], scalar2=math.pi / 2.0, op0=ALU.mult, op1=ALU.add
+        )
+    ang_flat = ang[:].rearrange("p a m j -> p (a m j)")
+    n = 2 * MT * ROT
+    turns_i = const.tile([P, n], I32, name="turns_i")
+    nc.vector.tensor_scalar(out=turns_i[:], in0=ang_flat, scalar1=1.0 / (2.0 * math.pi), scalar2=None, op0=ALU.mult)
+    turns = const.tile([P, n], F32, name="turns")
+    nc.vector.tensor_copy(out=turns[:], in_=turns_i[:])
+    return ang_flat, turns
+
+
+def rope_reduction_steps(nc, const, ang_flat, turns):
+    n = 2 * MT * ROT
+    c1 = 6.28125
+    c2 = 2.0 * math.pi - c1
+    red = const.tile([P, n], F32, name="red")
+    fix = const.tile([P, n], F32, name="fix")
+    return red, (
+        lambda: nc.vector.scalar_tensor_tensor(out=red[:], in0=turns[:], scalar=-c1, in1=ang_flat, op0=ALU.mult, op1=ALU.add),
+        lambda: nc.vector.scalar_tensor_tensor(out=red[:], in0=turns[:], scalar=-c2, in1=red[:], op0=ALU.mult, op1=ALU.add),
+        lambda: nc.vector.tensor_scalar(
+            out=fix[:], in0=red[:], scalar1=math.pi, scalar2=-2.0 * math.pi, op0=ALU.is_gt, op1=ALU.mult
+        ),
+        lambda: nc.vector.tensor_tensor(out=red[:], in0=red[:], in1=fix[:], op=ALU.add),
+    )
+
+
+def rope_tables(nc, const, red):
+    cs = const.tile([P, MT, 2, 2, ROT], F32, name="cs")
+    red4 = red[:].rearrange("p (a m j) -> p a m j", a=2, m=MT)
+    nc.scalar.activation(out=cs[:, :, 0, 0, :], in_=red4[:, 1], func=ACT.Sin)
+    nc.scalar.activation(out=cs[:, :, 0, 1, :], in_=red4[:, 1], func=ACT.Sin)
+    nc.scalar.activation(out=cs[:, :, 1, 0, :], in_=red4[:, 0], func=ACT.Sin, scale=-1.0)
+    nc.scalar.activation(out=cs[:, :, 1, 1, :], in_=red4[:, 0], func=ACT.Sin)
+    return cs
+
+
+def tile_groupedqueryattention_pa_kernel(tc, x, Wqkv_bytes, Wqkv_scale, out_0, out_1, out_2):
+    nc = tc.nc
+    steps = [(u, g) for u in range(len(UNITS)) for g in range(PASSES)]
+    w_view = Wqkv_bytes.rearrange("(g p t) n -> g p t n", p=P, t=PACK)
+    x_view = x.rearrange("(m p) k -> p m k", p=P)
+    outs = (
+        out_0.rearrange("l h d -> l (h d)"),
+        out_1.rearrange("l h d -> l (h d)"),
+        out_2.rearrange("l h d -> l (h d)"),
+    )
+
+    with ExitStack() as ctx:
+        const = ctx.enter_context(tc.tile_pool(name="const", bufs=1))
+        bytes_pool = ctx.enter_context(tc.tile_pool(name="bytes", bufs=1))
+        xpool = ctx.enter_context(tc.tile_pool(name="xpool", bufs=1))
+        shared = ctx.enter_context(tc.tile_pool(name="shared", bufs=1))
+        wide_pool = ctx.enter_context(tc.tile_pool(name="wide", bufs=4))
+        inter_pool = ctx.enter_context(tc.tile_pool(name="inter", bufs=3))
+        code_pool = ctx.enter_context(tc.tile_pool(name="code", bufs=4))
+        stage_pool = ctx.enter_context(tc.tile_pool(name="stage", bufs=4))
+        tmp_pool = ctx.enter_context(tc.tile_pool(name="tmp", bufs=4))
+        psum = ctx.enter_context(tc.psum_pool(name="psum", bufs=8))
+
+        zero = const.tile([P, 1], F32, name="zero")
+        nc.vector.memset(zero[:], 0.0)
+        junk = const.tile([P, 1], F32, name="junk")
+        nc.scalar.activation(out=junk[:], in_=zero[:], func=ACT.Sin)
+
+        wsc = const.tile([P, PASSES, PACK], F32, name="wsc")
+        nc.sync.dma_start(out=wsc[:], in_=Wqkv_scale.rearrange("(g p t) o -> p g (t o)", p=P, t=PACK))
+
+        wb = {}
+        xraw = []
+
+        def load_bytes(s):
+            u, g = steps[s]
+            c0, width = UNITS[u][1], UNITS[u][2]
+            t_ = bytes_pool.tile([P, PACK, width], U8, name="wb%d" % s)
+            nc.sync.dma_start(out=t_[:], in_=w_view[g][:, :, c0 : c0 + width])
+            wb[s] = [t_[:, t, :] for t in range(PACK)]
+
+        def load_plane(s, t):
+            u, g = steps[s]
+            c0, width = UNITS[u][1], UNITS[u][2]
+            t_ = bytes_pool.tile([P, width], U8, name="wb%d_%d" % (s, t))
+            nc.sync.dma_start(out=t_[:], in_=w_view[g][:, t, c0 : c0 + width])
+            wb.setdefault(s, {})[t] = t_[:]
+
+        def load_x(g):
+            t_ = shared.tile([P, MT, 512], BF16, name="xraw%d" % g, offset=g * 4096)
+            nc.sync.dma_start(out=t_[:], in_=x_view[:, :, g * 512 : (g + 1) * 512])
+            xraw.append(t_)
+
+        for s, t in HEAD_PLANES:
+            load_plane(s, t)
+        load_x(0)
+        load_x(1)
+        load_x(2)
+        load_x(3)
+        for s in range(2, len(steps)):
+            load_bytes(s)
+
+        ident = const.tile([P, P], F32, name="ident")
+        make_identity(nc, ident[:])
+
+        xc = xpool.tile([P, PASSES, 512], U32, name="xc", align_bytes=64)
+        xs = xpool.tile([P, PASSES, 512], U8, name="xs", align_bytes=64)
+
+        wide = {}
+        inter = {}
+        codes = {}
+        banks = {}
+
+        def widen_plane(s, t):
+            u, g = steps[s]
+            width = UNITS[u][2]
+            if s not in wide:
+                if width == 1024:
+                    wt = wide_pool.tile([P, PACK, width], BF16, tag="wide")
+                else:
+                    wt = shared.tile([P, PACK, width], BF16, name="widekv%d" % s, offset=(s - 8) * 4096)
+                wide[s] = wt
+            wt = wide[s]
+            src = wb[s][t].bitcast(FP8)
+            if (s, t) in V_WIDEN:
+                nc.vector.tensor_scalar(out=wt[:, t, :], in0=src, scalar1=wsc[:, g, t : t + 1], scalar2=None, op0=ALU.mult)
+            else:
+                nc.scalar.activation(out=wt[:, t, :], in_=src, func=ACT.Copy, scale=wsc[:, g, t : t + 1])
+
+        def widen(s):
+            for t in range(PACK):
+                widen_plane(s, t)
+
+        def interleave(s):
+            u, g = steps[s]
+            kind, width = UNITS[u][0], UNITS[u][2]
+            it = inter_pool.tile([P, PACK * width], BF16, tag="inter", align_bytes=64)
+            inter[s] = it
+            wt = wide[s]
+            if kind == "v":
+                dst = it[:].rearrange("p (c i t) -> p c t i", i=RUN, t=PACK)
+                src = wt[:].rearrange("p t (c i) -> p c t i", i=RUN)
+                if s in S_INTER:
+                    nc.scalar.copy(out=dst, in_=src)
+                else:
+                    nc.vector.tensor_copy(out=dst, in_=src)
+            else:
+                half = PACK * width // 2
+                src = wt[:].rearrange("p t (hh q c i) -> p q hh c t i", q=2, c=ROT // RUN, i=RUN)
+                for q in range(2):
+                    nc.vector.tensor_copy(
+                        out=it[:, q * half : (q + 1) * half].rearrange(
+                            "p (hh c i t) -> p hh c t i", c=ROT // RUN, i=RUN, t=PACK
+                        ),
+                        in_=src[:, q],
+                    )
+
+        def quantize(s):
+            u, g = steps[s]
+            width = UNITS[u][2]
+            cd = code_pool.tile([P, width], U32, tag="codes", align_bytes=64)
+            sc = code_pool.tile([P, width], U8, tag="scl", align_bytes=64)
+            codes[s] = (cd, sc)
+            nc.vector.quantize_mx(out=cd[:].bitcast(FP8X4), scales=sc[:], in_=inter[s][:])
+
+        def multiply(s):
+            u, g = steps[s]
+            width = UNITS[u][2]
+            nb = width // 512
+            if g == 0:
+                for b in reversed(range(nb)):
+                    for m in range(MT):
+                        bank = psum.tile([P, 512], F32, tag="bank")
+                        banks[(u, m, b)] = bank
+            cd, sc = codes[s]
+            for m in range(MT):
+                for b in range(nb):
+                    nc.tensor.matmul_mx(
+                        out=banks[(u, m, b)][:],
+                        lhsT=xc[:, g, m * P : (m + 1) * P].bitcast(FP8X4),
+                        lhsT_scale=xs[:, g, m * P : (m + 1) * P],
+                        rhs=cd[:, b * 512 : (b + 1) * 512].bitcast(FP8X4),
+                        rhs_scale=sc[:, b * 512 : (b + 1) * 512],
+                        start=(g == 0),
+                        stop=(g == PASSES - 1),
+                    )
+
+        products = {}
+
+        def rope_products(key, rot_src, m, heads):
+            tmp = tmp_pool.tile([P, 2, heads, 2, ROT], F32, tag="tmp")
+            products[key] = tmp
+            nc.vector.tensor_tensor(
+                out=tmp[:].rearrange("p a h f j -> p a h (f j)"),
+                in0=rot_src.rearrange("p (h fj) -> p h fj", fj=2 * ROT).unsqueeze(1).to_broadcast([P, 2, heads, 2 * ROT]),
+                in1=cs[:, m].rearrange("p a f j -> p a (f j)").unsqueeze(2).to_broadcast([P, 2, heads, 2 * ROT]),
+                op=ALU.mult,
+            )
+
+        def rope_sum(key, st):
+            tmp = products[key]
+            st5 = st.rearrange("p (h f q j) -> p h f q j", f=2, q=2, j=ROT)
+            eng = nc.gpsimd if key[1] in G_SUMS else nc.vector
+            eng.tensor_tensor(out=st5[:, :, :, 0, :], in0=tmp[:, 0], in1=tmp[:, 1][:, :, ::-1, :], op=ALU.add)
+
+        stages = {}
+
+        def epilogue_scalar(u, m):
+            kind, c0, width = UNITS[u]
+            st = stage_pool.tile([P, width], F32, tag="stage_" + kind)
+            stages[(u, m)] = st
+            if kind == "q":
+                nc.scalar.copy(
+                    out=st[:].rearrange("p (hh q j) -> p hh q j", q=2, j=ROT)[:, :, 1, :],
+                    in_=banks[(u, m, 1)][:].rearrange("p (hh j) -> p hh j", j=ROT),
+                )
+            elif kind == "k":
+                nc.scalar.copy(
+                    out=st[:].rearrange("p (hh q j) -> p hh q j", q=2, j=ROT)[:, :, 1, :],
+                    in_=banks[(u, m, 0)][:, 256:512].rearrange("p (hh j) -> p hh j", j=ROT),
+                )
+            else:
+                nc.scalar.copy(out=st[:], in_=banks[(u, m, 0)][:])
+
+        def epilogue_products(u, m):
+            if UNITS[u][0] == "q":
+                rope_products((u, m), banks[(u, m, 0)][:], m, 8)
+            else:
+                rope_products((u, m), banks[(u, m, 0)][:, 0:256], m, 4)
+
+        def epilogue_finish(u, m):
+            kind, c0, width = UNITS[u]
+            st = stages[(u, m)]
+            rows = slice(m * P, (m + 1) * P)
+            if kind == "q":
+                rope_sum((u, m), st[:])
+                nc.sync.dma_start(out=outs[0][rows, c0 : c0 + width], in_=st[:])
+            elif kind == "k":
+                rope_sum((u, m), st[:])
+                nc.sync.dma_start(out=outs[1][rows, :], in_=st[:])
+            else:
+                nc.scalar.dma_start(out=outs[2][rows, :], in_=st[:])
+
+        def epilogue_vector_all(u):
+            for m in range(MT):
+                epilogue_products(u, m)
+            for m in range(MT):
+                epilogue_finish(u, m)
+
+        xg = []
+
+        def x_turn(g):
+            gt = shared.tile([P, MT * P * PACK], BF16, name="xg%d" % g, align_bytes=64, offset=(PASSES + g) * 4096)
+            xg.append(gt)
+            for h in range(2):
+                xt = psum.tile([P, 4, P], F32, tag="bank")
+                for mm in range(2):
+                    words = xraw[g][:, 2 * h + mm, :].bitcast(F32)
+                    for e in range(2):
+                        nc.tensor.transpose(xt[:, 2 * mm + e, :], words[:, e : 256 : 2], ident[:])
+                dst = gt[:, h * 1024 : (h + 1) * 1024].bitcast(F32).rearrange("p (mm r e) -> p mm r e", mm=2, e=2)
+                src = xt[:].rearrange("p (mm e) r -> p mm r e", e=2)
+                if 2 * g + h in X_EVAC_ON_S:
+                    nc.scalar.copy(out=dst, in_=src)
+                else:
+                    nc.vector.tensor_copy(out=dst, in_=src)
+
+        def x_quant(g):
+            nc.vector.quantize_mx(out=xc[:, g, :].bitcast(FP8X4), scales=xs[:, g, :], in_=xg[g][:])
+
+        widen_plane(1, 0)
+        widen_plane(1, 1)
+        ang_flat, turns = rope_angles(nc, const)
+        red, reduction = rope_reduction_steps(nc, const, ang_flat, turns)
+        for t in range(PACK):
+            widen_plane(0, t)
+            reduction[t]()
+        widen_plane(1, 2)
+        widen_plane(1, 3)
+        x_turn(0)
+        x_turn(1)
+        interleave(0)
+        x_quant(0)
+        x_turn(2)
+        x_quant(1)
+        x_turn(3)
+        x_quant(2)
+        x_quant(3)
+        cs = rope_tables(nc, const, red)
+
+        n = len(steps)
+        for i in range(2, n + 2):
+            if i < n:
+                widen(i)
+            if i == n - 1:
+                for m in range(MT):
+                    epilogue_scalar(2, m)
+            if i - 1 < n:
+                interleave(i - 1)
+            quantize(i - 2)
+            multiply(i - 2)
+            u, g = steps[i - 2]
+            if g == PASSES - 1 and u < 2:
+                for m in range(MT):
+                    epilogue_scalar(u, m)
+                epilogue_vector_all(u)
+        for m in range(MT):
+            epilogue_scalar(3, m)
+            epilogue_finish(3, m)
+        epilogue_vector_all(2)

@@ -21,7 +21,7 @@ PACK = 4
 PASSES = 4
 MT = 4
 ROT = 32
-RUN = 4
+RUN = 8
 
 UNITS = (("q", 0, 1024), ("q", 1024, 1024), ("k", 2048, 512), ("v", 2560, 512))
 

@@ -24,64 +24,51 @@ ROT = 32
 RUN = 8
 
 UNITS = (("q", 0, 1024), ("q", 1024, 1024), ("k", 2048, 512), ("v", 2560, 512))
+STEPS = tuple((u, g) for u in range(len(UNITS)) for g in range(PASSES))
+N_STEPS = len(STEPS)
 
-V_WIDEN = {(0, 0), (0, 1), (0, 2), (0, 3), (1, 2), (1, 3), (2, 3), (3, 3)}
-S_INTER = (15,)
+V_PLANES = {(0, 0), (0, 1), (0, 2), (0, 3), (1, 3), (2, 3), (3, 3), (4, 3)}
 HEAD_PLANES = ((1, 0), (0, 0), (0, 1), (1, 1), (0, 2), (0, 3), (1, 2), (1, 3))
-G_SUMS = (0, 1)
-X_EVAC_ON_S = (0, 1, 2, 3, 4, 5, 6, 7)
+S_HALVES = {(8, 0), (12, 0), (15, 0), (15, 1)}
+COPY_STEP = {6: 0, 12: 1}
 
 
 def rope_angles(nc, const):
-    pos_i = const.tile([P, MT], I32, name="pos_i")
-    nc.gpsimd.iota(pos_i[:], pattern=[[P, MT]], base=0, channel_multiplier=1)
-    freq = const.tile([P, ROT], F32, name="freq")
-    nc.vector.memset(freq[:], 1.0)
-    pos = const.tile([P, MT], F32, name="pos")
-    nc.vector.tensor_copy(out=pos[:], in_=pos_i[:])
-    for w in (1, 4, 16):
-        for r in range(1, min(4, ROT // w)):
-            nc.vector.tensor_scalar(
-                out=freq[:, r * w : (r + 1) * w],
-                in0=freq[:, 0:w],
-                scalar1=(1.0 / 1024.0) ** (r * w / 31.0),
-                scalar2=None,
-                op0=ALU.mult,
-            )
-    ang = const.tile([P, 2, MT, ROT], F32, name="ang")
-    for m in range(MT):
-        nc.vector.tensor_scalar(out=ang[:, 0, m, :], in0=freq[:], scalar1=pos[:, m : m + 1], scalar2=None, op0=ALU.mult)
+    pos = const.tile([P, MT], I32, name="pos")
+    nc.gpsimd.iota(pos[:], pattern=[[P, MT]], base=0, channel_multiplier=1)
+    ang = const.tile([P, 2, ROT, MT], F32, name="ang")
+
+    def factor(j):
+        return (1.0 / 1024.0) ** (j / 31.0)
+
+    for j in range(4):
+        nc.vector.tensor_scalar(out=ang[:, 0, j, :], in0=pos[:], scalar1=factor(j), scalar2=None, op0=ALU.mult)
+    for j in (4, 8, 12):
         nc.vector.tensor_scalar(
-            out=ang[:, 1, m, :], in0=freq[:], scalar1=pos[:, m : m + 1], scalar2=math.pi / 2.0, op0=ALU.mult, op1=ALU.add
+            out=ang[:, 0, j : j + 4, :], in0=ang[:, 0, 0:4, :], scalar1=factor(j), scalar2=None, op0=ALU.mult
         )
-    ang_flat = ang[:].rearrange("p a m j -> p (a m j)")
+    low = ang[:, 0, 0:16, :]
+    nc.vector.tensor_scalar(out=ang[:, 0, 16:32, :], in0=low, scalar1=factor(16), scalar2=None, op0=ALU.mult)
+    for j in (0, 16):
+        nc.vector.tensor_scalar(
+            out=ang[:, 1, j : j + 16, :], in0=low, scalar1=factor(j), scalar2=math.pi / 2.0, op0=ALU.mult, op1=ALU.add
+        )
+    ang_flat = ang[:].rearrange("p a j m -> p (a j m)")
     n = 2 * MT * ROT
-    turns_i = const.tile([P, n], I32, name="turns_i")
-    nc.vector.tensor_scalar(out=turns_i[:], in0=ang_flat, scalar1=1.0 / (2.0 * math.pi), scalar2=None, op0=ALU.mult)
-    turns = const.tile([P, n], F32, name="turns")
-    nc.vector.tensor_copy(out=turns[:], in_=turns_i[:])
-    return ang_flat, turns
-
-
-def rope_reduction_steps(nc, const, ang_flat, turns):
-    n = 2 * MT * ROT
+    turns = const.tile([P, n], I32, name="turns")
+    nc.vector.tensor_scalar(out=turns[:], in0=ang_flat, scalar1=1.0 / (2.0 * math.pi), scalar2=None, op0=ALU.mult)
     c1 = 6.28125
     c2 = 2.0 * math.pi - c1
+    part = const.tile([P, n], F32, name="part")
+    nc.vector.scalar_tensor_tensor(out=part[:], in0=turns[:], scalar=-c1, in1=ang_flat, op0=ALU.mult, op1=ALU.add)
     red = const.tile([P, n], F32, name="red")
-    fix = const.tile([P, n], F32, name="fix")
-    return red, (
-        lambda: nc.vector.scalar_tensor_tensor(out=red[:], in0=turns[:], scalar=-c1, in1=ang_flat, op0=ALU.mult, op1=ALU.add),
-        lambda: nc.vector.scalar_tensor_tensor(out=red[:], in0=turns[:], scalar=-c2, in1=red[:], op0=ALU.mult, op1=ALU.add),
-        lambda: nc.vector.tensor_scalar(
-            out=fix[:], in0=red[:], scalar1=math.pi, scalar2=-2.0 * math.pi, op0=ALU.is_gt, op1=ALU.mult
-        ),
-        lambda: nc.vector.tensor_tensor(out=red[:], in0=red[:], in1=fix[:], op=ALU.add),
-    )
+    nc.vector.scalar_tensor_tensor(out=red[:], in0=turns[:], scalar=-c2, in1=part[:], op0=ALU.mult, op1=ALU.add)
+    return red
 
 
 def rope_tables(nc, const, red):
     cs = const.tile([P, MT, 2, 2, ROT], F32, name="cs")
-    red4 = red[:].rearrange("p (a m j) -> p a m j", a=2, m=MT)
+    red4 = red[:].rearrange("p (a j m) -> p a m j", a=2, m=MT)
     nc.scalar.activation(out=cs[:, :, 0, 0, :], in_=red4[:, 1], func=ACT.Sin)
     nc.scalar.activation(out=cs[:, :, 0, 1, :], in_=red4[:, 1], func=ACT.Sin)
     nc.scalar.activation(out=cs[:, :, 1, 0, :], in_=red4[:, 0], func=ACT.Sin, scale=-1.0)
@@ -91,14 +78,10 @@ def rope_tables(nc, const, red):
 
 def tile_groupedqueryattention_pa_kernel(tc, x, Wqkv_bytes, Wqkv_scale, out_0, out_1, out_2):
     nc = tc.nc
-    steps = [(u, g) for u in range(len(UNITS)) for g in range(PASSES)]
     w_view = Wqkv_bytes.rearrange("(g p t) n -> g p t n", p=P, t=PACK)
     x_view = x.rearrange("(m p) k -> p m k", p=P)
-    outs = (
-        out_0.rearrange("l h d -> l (h d)"),
-        out_1.rearrange("l h d -> l (h d)"),
-        out_2.rearrange("l h d -> l (h d)"),
-    )
+    out_q, out_k, out_v = (o.rearrange("l h d -> l (h d)") for o in (out_0, out_1, out_2))
+    out_of = {"q": out_q, "k": out_k, "v": out_v}
 
     with ExitStack() as ctx:
         const = ctx.enter_context(tc.tile_pool(name="const", bufs=1))
@@ -111,6 +94,7 @@ def tile_groupedqueryattention_pa_kernel(tc, x, Wqkv_bytes, Wqkv_scale, out_0, o
         stage_pool = ctx.enter_context(tc.tile_pool(name="stage", bufs=4))
         tmp_pool = ctx.enter_context(tc.tile_pool(name="tmp", bufs=4))
         psum = ctx.enter_context(tc.psum_pool(name="psum", bufs=8))
+        ctx.enter_context(tc.manual_schedule())
 
         zero = const.tile([P, 1], F32, name="zero")
         nc.vector.memset(zero[:], 0.0)
@@ -124,14 +108,14 @@ def tile_groupedqueryattention_pa_kernel(tc, x, Wqkv_bytes, Wqkv_scale, out_0, o
         xraw = []
 
         def load_bytes(s):
-            u, g = steps[s]
+            u, g = STEPS[s]
             c0, width = UNITS[u][1], UNITS[u][2]
             t_ = bytes_pool.tile([P, PACK, width], U8, name="wb%d" % s)
             nc.sync.dma_start(out=t_[:], in_=w_view[g][:, :, c0 : c0 + width])
             wb[s] = [t_[:, t, :] for t in range(PACK)]
 
         def load_plane(s, t):
-            u, g = steps[s]
+            u, g = STEPS[s]
             c0, width = UNITS[u][1], UNITS[u][2]
             t_ = bytes_pool.tile([P, width], U8, name="wb%d_%d" % (s, t))
             nc.sync.dma_start(out=t_[:], in_=w_view[g][:, t, c0 : c0 + width])
@@ -144,12 +128,12 @@ def tile_groupedqueryattention_pa_kernel(tc, x, Wqkv_bytes, Wqkv_scale, out_0, o
 
         for s, t in HEAD_PLANES:
             load_plane(s, t)
-        load_x(0)
-        load_x(1)
-        load_x(2)
-        load_x(3)
-        for s in range(2, len(steps)):
+        for g in range(PASSES):
+            load_x(g)
+        for s in range(2, N_STEPS):
             load_bytes(s)
+
+        red = rope_angles(nc, const)
 
         ident = const.tile([P, P], F32, name="ident")
         make_identity(nc, ident[:])
@@ -163,7 +147,7 @@ def tile_groupedqueryattention_pa_kernel(tc, x, Wqkv_bytes, Wqkv_scale, out_0, o
         banks = {}
 
         def widen_plane(s, t):
-            u, g = steps[s]
+            u, g = STEPS[s]
             width = UNITS[u][2]
             if s not in wide:
                 if width == 1024:
@@ -173,7 +157,7 @@ def tile_groupedqueryattention_pa_kernel(tc, x, Wqkv_bytes, Wqkv_scale, out_0, o
                 wide[s] = wt
             wt = wide[s]
             src = wb[s][t].bitcast(FP8)
-            if (s, t) in V_WIDEN:
+            if (s, t) in V_PLANES:
                 nc.vector.tensor_scalar(out=wt[:, t, :], in0=src, scalar1=wsc[:, g, t : t + 1], scalar2=None, op0=ALU.mult)
             else:
                 nc.scalar.activation(out=wt[:, t, :], in_=src, func=ACT.Copy, scale=wsc[:, g, t : t + 1])
@@ -183,43 +167,37 @@ def tile_groupedqueryattention_pa_kernel(tc, x, Wqkv_bytes, Wqkv_scale, out_0, o
                 widen_plane(s, t)
 
         def interleave(s):
-            u, g = steps[s]
+            u, g = STEPS[s]
             kind, width = UNITS[u][0], UNITS[u][2]
             it = inter_pool.tile([P, PACK * width], BF16, tag="inter", align_bytes=64)
             inter[s] = it
             wt = wide[s]
-            if kind == "v":
-                dst = it[:].rearrange("p (c i t) -> p c t i", i=RUN, t=PACK)
-                src = wt[:].rearrange("p t (c i) -> p c t i", i=RUN)
-                if s in S_INTER:
+            half = PACK * width // 2
+            for q in range(2):
+                dst = it[:, q * half : (q + 1) * half]
+                if kind == "v":
+                    dst = dst.rearrange("p (c i t) -> p c t i", i=RUN, t=PACK)
+                    src = wt[:, :, q * width // 2 : (q + 1) * width // 2].rearrange("p t (c i) -> p c t i", i=RUN)
+                else:
+                    dst = dst.rearrange("p (hh c i t) -> p hh c t i", c=ROT // RUN, i=RUN, t=PACK)
+                    src = wt[:].rearrange("p t (hh q c i) -> p q hh c t i", q=2, c=ROT // RUN, i=RUN)[:, q]
+                if (s, q) in S_HALVES:
                     nc.scalar.copy(out=dst, in_=src)
                 else:
                     nc.vector.tensor_copy(out=dst, in_=src)
-            else:
-                half = PACK * width // 2
-                src = wt[:].rearrange("p t (hh q c i) -> p q hh c t i", q=2, c=ROT // RUN, i=RUN)
-                for q in range(2):
-                    nc.vector.tensor_copy(
-                        out=it[:, q * half : (q + 1) * half].rearrange(
-                            "p (hh c i t) -> p hh c t i", c=ROT // RUN, i=RUN, t=PACK
-                        ),
-                        in_=src[:, q],
-                    )
 
         def quantize(s):
-            u, g = steps[s]
-            width = UNITS[u][2]
+            width = UNITS[STEPS[s][0]][2]
             cd = code_pool.tile([P, width], U32, tag="codes", align_bytes=64)
             sc = code_pool.tile([P, width], U8, tag="scl", align_bytes=64)
             codes[s] = (cd, sc)
             nc.vector.quantize_mx(out=cd[:].bitcast(FP8X4), scales=sc[:], in_=inter[s][:])
 
         def multiply(s):
-            u, g = steps[s]
-            width = UNITS[u][2]
-            nb = width // 512
+            u, g = STEPS[s]
+            nb = UNITS[u][2] // 512
             if g == 0:
-                for b in reversed(range(nb)):
+                for b in range(nb):
                     for m in range(MT):
                         bank = psum.tile([P, 512], F32, tag="bank")
                         banks[(u, m, b)] = bank
@@ -236,67 +214,50 @@ def tile_groupedqueryattention_pa_kernel(tc, x, Wqkv_bytes, Wqkv_scale, out_0, o
                         stop=(g == PASSES - 1),
                     )
 
+        stages = {}
         products = {}
 
-        def rope_products(key, rot_src, m, heads):
+        def stage(u, m):
+            if (u, m) not in stages:
+                kind, width = UNITS[u][0], UNITS[u][2]
+                st = stage_pool.tile([P, width], F32, tag="stage_" + kind)
+                stages[(u, m)] = st
+            return stages[(u, m)]
+
+        def copy_out(u, m):
+            kind = UNITS[u][0]
+            st = stage(u, m)
+            if kind == "v":
+                nc.scalar.copy(out=st[:], in_=banks[(u, m, 0)][:])
+            else:
+                src = banks[(u, m, 1)][:] if kind == "q" else banks[(u, m, 0)][:, 256:512]
+                nc.scalar.copy(
+                    out=st[:].rearrange("p (hh q j) -> p hh q j", q=2, j=ROT)[:, :, 1, :],
+                    in_=src.rearrange("p (hh j) -> p hh j", j=ROT),
+                )
+
+        def rope_products(u, m):
+            heads = UNITS[u][2] // 128
+            src = banks[(u, m, 0)][:, 0 : heads * 2 * ROT]
             tmp = tmp_pool.tile([P, 2, heads, 2, ROT], F32, tag="tmp")
-            products[key] = tmp
+            products[(u, m)] = tmp
             nc.vector.tensor_tensor(
                 out=tmp[:].rearrange("p a h f j -> p a h (f j)"),
-                in0=rot_src.rearrange("p (h fj) -> p h fj", fj=2 * ROT).unsqueeze(1).to_broadcast([P, 2, heads, 2 * ROT]),
+                in0=src.rearrange("p (h fj) -> p h fj", fj=2 * ROT).unsqueeze(1).to_broadcast([P, 2, heads, 2 * ROT]),
                 in1=cs[:, m].rearrange("p a f j -> p a (f j)").unsqueeze(2).to_broadcast([P, 2, heads, 2 * ROT]),
                 op=ALU.mult,
             )
 
-        def rope_sum(key, st):
-            tmp = products[key]
-            st5 = st.rearrange("p (h f q j) -> p h f q j", f=2, q=2, j=ROT)
-            eng = nc.gpsimd if key[1] in G_SUMS else nc.vector
+        def rope_sum(u, m):
+            tmp = products[(u, m)]
+            st5 = stage(u, m)[:].rearrange("p (h f q j) -> p h f q j", f=2, q=2, j=ROT)
+            eng = nc.gpsimd if m < 2 else nc.vector
             eng.tensor_tensor(out=st5[:, :, :, 0, :], in0=tmp[:, 0], in1=tmp[:, 1][:, :, ::-1, :], op=ALU.add)
 
-        stages = {}
-
-        def epilogue_scalar(u, m):
+        def store(u, m):
             kind, c0, width = UNITS[u]
-            st = stage_pool.tile([P, width], F32, tag="stage_" + kind)
-            stages[(u, m)] = st
-            if kind == "q":
-                nc.scalar.copy(
-                    out=st[:].rearrange("p (hh q j) -> p hh q j", q=2, j=ROT)[:, :, 1, :],
-                    in_=banks[(u, m, 1)][:].rearrange("p (hh j) -> p hh j", j=ROT),
-                )
-            elif kind == "k":
-                nc.scalar.copy(
-                    out=st[:].rearrange("p (hh q j) -> p hh q j", q=2, j=ROT)[:, :, 1, :],
-                    in_=banks[(u, m, 0)][:, 256:512].rearrange("p (hh j) -> p hh j", j=ROT),
-                )
-            else:
-                nc.scalar.copy(out=st[:], in_=banks[(u, m, 0)][:])
-
-        def epilogue_products(u, m):
-            if UNITS[u][0] == "q":
-                rope_products((u, m), banks[(u, m, 0)][:], m, 8)
-            else:
-                rope_products((u, m), banks[(u, m, 0)][:, 0:256], m, 4)
-
-        def epilogue_finish(u, m):
-            kind, c0, width = UNITS[u]
-            st = stages[(u, m)]
-            rows = slice(m * P, (m + 1) * P)
-            if kind == "q":
-                rope_sum((u, m), st[:])
-                nc.sync.dma_start(out=outs[0][rows, c0 : c0 + width], in_=st[:])
-            elif kind == "k":
-                rope_sum((u, m), st[:])
-                nc.sync.dma_start(out=outs[1][rows, :], in_=st[:])
-            else:
-                nc.scalar.dma_start(out=outs[2][rows, :], in_=st[:])
-
-        def epilogue_vector_all(u):
-            for m in range(MT):
-                epilogue_products(u, m)
-            for m in range(MT):
-                epilogue_finish(u, m)
+            c0 = c0 if kind == "q" else 0
+            nc.sync.dma_start(out=out_of[kind][m * P : (m + 1) * P, c0 : c0 + width], in_=stages[(u, m)][:])
 
         xg = []
 
@@ -309,53 +270,82 @@ def tile_groupedqueryattention_pa_kernel(tc, x, Wqkv_bytes, Wqkv_scale, out_0, o
                     words = xraw[g][:, 2 * h + mm, :].bitcast(F32)
                     for e in range(2):
                         nc.tensor.transpose(xt[:, 2 * mm + e, :], words[:, e : 256 : 2], ident[:])
-                dst = gt[:, h * 1024 : (h + 1) * 1024].bitcast(F32).rearrange("p (mm r e) -> p mm r e", mm=2, e=2)
-                src = xt[:].rearrange("p (mm e) r -> p mm r e", e=2)
-                if 2 * g + h in X_EVAC_ON_S:
-                    nc.scalar.copy(out=dst, in_=src)
-                else:
-                    nc.vector.tensor_copy(out=dst, in_=src)
+                nc.scalar.copy(
+                    out=gt[:, h * 1024 : (h + 1) * 1024].bitcast(F32).rearrange("p (mm r e) -> p mm r e", mm=2, e=2),
+                    in_=xt[:].rearrange("p (mm e) r -> p mm r e", e=2),
+                )
 
         def x_quant(g):
             nc.vector.quantize_mx(out=xc[:, g, :].bitcast(FP8X4), scales=xs[:, g, :], in_=xg[g][:])
 
-        widen_plane(1, 0)
-        widen_plane(1, 1)
-        ang_flat, turns = rope_angles(nc, const)
-        red, reduction = rope_reduction_steps(nc, const, ang_flat, turns)
-        for t in range(PACK):
-            widen_plane(0, t)
-            reduction[t]()
-        widen_plane(1, 2)
-        widen_plane(1, 3)
-        x_turn(0)
-        x_turn(1)
+        widen(0)
+        widen(1)
+        for g in range(PASSES):
+            x_turn(g)
         interleave(0)
-        x_quant(0)
-        x_turn(2)
-        x_quant(1)
-        x_turn(3)
-        x_quant(2)
-        x_quant(3)
-        cs = rope_tables(nc, const, red)
+        interleave(1)
+        for g in range(PASSES):
+            x_quant(g)
+        copied = set()
+        rotated = set()
+        waiting = []
 
-        n = len(steps)
-        for i in range(2, n + 2):
-            if i < n:
-                widen(i)
-            if i == n - 1:
+        def banks_are_read(s):
+            u, g = STEPS[s]
+            if g > 0 or u == 0:
+                return True
+            if u == 1:
+                return 0 in copied and 0 in rotated
+            return 1 in (rotated if u == 2 else copied)
+
+        for i in range(2, N_STEPS):
+            widen(i)
+            if i == 2:
+                cs = rope_tables(nc, const, red)
+            if i in COPY_STEP:
+                u = COPY_STEP[i]
                 for m in range(MT):
-                    epilogue_scalar(2, m)
-            if i - 1 < n:
+                    copy_out(u, m)
+                copied.add(u)
+                if u in rotated:
+                    for m in range(MT):
+                        store(u, m)
+            if i > 2:
                 interleave(i - 1)
-            quantize(i - 2)
-            multiply(i - 2)
-            u, g = steps[i - 2]
-            if g == PASSES - 1 and u < 2:
+            if i in (6, 10):
+                u = i // 4 - 1
                 for m in range(MT):
-                    epilogue_scalar(u, m)
-                epilogue_vector_all(u)
+                    rope_products(u, m)
+                rotated.add(u)
+                for m in range(MT):
+                    rope_sum(u, m)
+                if u in copied:
+                    for m in range(MT):
+                        store(u, m)
+            quantize(i - 2)
+            waiting.append(i - 2)
+            while waiting and banks_are_read(waiting[0]):
+                multiply(waiting.pop(0))
+
+        interleave(15)
+        quantize(14)
+        multiply(14)
+        for m in (0, 1):
+            rope_products(2, m)
         for m in range(MT):
-            epilogue_scalar(3, m)
-            epilogue_finish(3, m)
-        epilogue_vector_all(2)
+            copy_out(2, m)
+        for m in (0, 1):
+            rope_sum(2, m)
+            store(2, m)
+        quantize(15)
+        multiply(15)
+        for m in (2, 3):
+            rope_products(2, m)
+        for m in (0, 1):
+            copy_out(3, m)
+            store(3, m)
+            rope_sum(2, m + 2)
+            store(2, m + 2)
+        for m in (2, 3):
+            copy_out(3, m)
+            store(3, m)

@@ -257,7 +257,8 @@ def tile_groupedqueryattention_pa_kernel(tc, x, Wqkv_bytes, Wqkv_scale, out_0, o
         def store(u, m):
             kind, c0, width = UNITS[u]
             c0 = c0 if kind == "q" else 0
-            nc.sync.dma_start(out=out_of[kind][m * P : (m + 1) * P, c0 : c0 + width], in_=stages[(u, m)][:])
+            queue = nc.scalar if kind == "v" else nc.sync
+            queue.dma_start(out=out_of[kind][m * P : (m + 1) * P, c0 : c0 + width], in_=stages[(u, m)][:])
 
         xg = []
 
@@ -341,11 +342,11 @@ def tile_groupedqueryattention_pa_kernel(tc, x, Wqkv_bytes, Wqkv_scale, out_0, o
         multiply(15)
         for m in (2, 3):
             rope_products(2, m)
-        for m in (0, 1):
-            copy_out(3, m)
-            store(3, m)
-            rope_sum(2, m + 2)
-            store(2, m + 2)
         for m in (2, 3):
+            rope_sum(2, m)
+            store(2, m)
+        for m in range(MT):
             copy_out(3, m)
-            store(3, m)
+            if m > 0:
+                store(3, m - 1)
+        store(3, MT - 1)

@@ -28,7 +28,7 @@ STEPS = tuple((u, g) for u in range(len(UNITS)) for g in range(PASSES))
 N_STEPS = len(STEPS)
 
 V_PLANES = {(0, 0), (0, 1), (0, 2), (0, 3), (1, 3), (2, 3), (3, 3), (4, 3)}
-HEAD_PLANES = ((1, 0), (0, 0), (0, 1), (1, 1), (0, 2), (0, 3), (1, 2), (1, 3))
+HEAD_PLANES = ((1, 0), (0, 0), (0, 1), (1, 1), (0, 2), (0, 3), (1, 2), (1, 3), (2, 0), (2, 3), (2, 1), (2, 2))
 S_HALVES = {(8, 0), (12, 0), (15, 0), (15, 1)}
 COPY_STEP = {6: 0, 12: 1}
 
@@ -128,9 +128,10 @@ def tile_groupedqueryattention_pa_kernel(tc, x, Wqkv_bytes, Wqkv_scale, out_0, o
 
         for s, t in HEAD_PLANES:
             load_plane(s, t)
+        load_bytes(3)
         for g in range(PASSES):
             load_x(g)
-        for s in range(2, N_STEPS):
+        for s in range(4, N_STEPS):
             load_bytes(s)
 
         red = rope_angles(nc, const)
@@ -281,12 +282,8 @@ def tile_groupedqueryattention_pa_kernel(tc, x, Wqkv_bytes, Wqkv_scale, out_0, o
 
         widen(0)
         widen(1)
-        for g in range(PASSES):
-            x_turn(g)
         interleave(0)
         interleave(1)
-        for g in range(PASSES):
-            x_quant(g)
         copied = set()
         rotated = set()
         waiting = []
@@ -301,7 +298,9 @@ def tile_groupedqueryattention_pa_kernel(tc, x, Wqkv_bytes, Wqkv_scale, out_0, o
 
         for i in range(2, N_STEPS):
             widen(i)
-            if i == 2:
+            if i == 3:
+                for g in range(PASSES):
+                    x_turn(g)
                 cs = rope_tables(nc, const, red)
             if i in COPY_STEP:
                 u = COPY_STEP[i]
@@ -323,9 +322,12 @@ def tile_groupedqueryattention_pa_kernel(tc, x, Wqkv_bytes, Wqkv_scale, out_0, o
                 if u in copied:
                     for m in range(MT):
                         store(u, m)
+            if i == 4:
+                for g in range(PASSES):
+                    x_quant(g)
             quantize(i - 2)
             waiting.append(i - 2)
-            while waiting and banks_are_read(waiting[0]):
+            while i >= 4 and waiting and banks_are_read(waiting[0]):
                 multiply(waiting.pop(0))
 
         interleave(15)

@@ -29,7 +29,7 @@ N_STEPS = len(STEPS)
 
 V_PLANES = {(0, 0), (0, 1), (0, 2), (0, 3), (1, 3), (2, 3), (3, 3), (4, 3)}
 HEAD_PLANES = ((1, 0), (0, 0), (0, 1), (1, 1), (0, 2), (0, 3), (1, 2), (1, 3), (2, 0), (2, 3), (2, 1), (2, 2))
-S_HALVES = {(8, 0), (12, 0), (15, 0), (15, 1)}
+S_HALVES = {(8, 0), (10, 0), (12, 0), (15, 0)}
 COPY_STEP = {6: 0, 12: 1}
 
 
@@ -232,7 +232,8 @@ def tile_groupedqueryattention_pa_kernel(tc, x, Wqkv_bytes, Wqkv_scale, out_0, o
                 nc.scalar.copy(out=st[:], in_=banks[(u, m, 0)][:])
             else:
                 src = banks[(u, m, 1)][:] if kind == "q" else banks[(u, m, 0)][:, 256:512]
-                nc.scalar.copy(
+                eng = nc.vector.tensor_copy if kind == "q" and m == MT - 1 else nc.scalar.copy
+                eng(
                     out=st[:].rearrange("p (hh q j) -> p hh q j", q=2, j=ROT)[:, :, 1, :],
                     in_=src.rearrange("p (hh j) -> p hh j", j=ROT),
                 )
@@ -252,7 +253,7 @@ def tile_groupedqueryattention_pa_kernel(tc, x, Wqkv_bytes, Wqkv_scale, out_0, o
         def rope_sum(u, m):
             tmp = products[(u, m)]
             st5 = stage(u, m)[:].rearrange("p (h f q j) -> p h f q j", f=2, q=2, j=ROT)
-            eng = nc.gpsimd if m < 2 else nc.vector
+            eng = nc.gpsimd if m < (3 if u < 2 else 2) else nc.vector
             eng.tensor_tensor(out=st5[:, :, :, 0, :], in0=tmp[:, 0], in1=tmp[:, 1][:, :, ::-1, :], op=ALU.add)
 
         def store(u, m):
@@ -304,7 +305,7 @@ def tile_groupedqueryattention_pa_kernel(tc, x, Wqkv_bytes, Wqkv_scale, out_0, o
                 cs = rope_tables(nc, const, red)
             if i in COPY_STEP:
                 u = COPY_STEP[i]
-                for m in range(MT):
+                for m in range(MT - 1):
                     copy_out(u, m)
                 copied.add(u)
                 if u in rotated:
@@ -316,6 +317,7 @@ def tile_groupedqueryattention_pa_kernel(tc, x, Wqkv_bytes, Wqkv_scale, out_0, o
                 u = i // 4 - 1
                 for m in range(MT):
                     rope_products(u, m)
+                copy_out(u, MT - 1)
                 rotated.add(u)
                 for m in range(MT):
                     rope_sum(u, m)

import math
from contextlib import ExitStack

import concourse.mybir as mybir
from concourse.masks import make_identity

FLOPS = 2 * 512 * 2048 * 3072

F32 = mybir.dt.float32
BF16 = mybir.dt.bfloat16
I32 = mybir.dt.int32
U32 = mybir.dt.uint32
U8 = mybir.dt.uint8
FP8 = mybir.dt.float8_e4m3fn
FP8X4 = mybir.dt.float8_e4m3fn_x4
ALU = mybir.AluOpType
ACT = mybir.ActivationFunctionType

P = 128
PACK = 4
PASSES = 4
MT = 4
ROT = 32
RUN = 8

UNITS = (("q", 0, 1024), ("q", 1024, 1024), ("k", 2048, 512), ("v", 2560, 512))
STEPS = tuple((u, g) for u in range(len(UNITS)) for g in range(PASSES))
N_STEPS = len(STEPS)

V_PLANES = {(0, 0), (0, 1), (0, 2), (0, 3), (1, 3), (2, 3), (3, 3), (4, 3)}
HEAD_PLANES = ((1, 0), (0, 0), (0, 1), (1, 1), (0, 2), (0, 3), (1, 2), (1, 3), (2, 0), (2, 3), (2, 1), (2, 2))
S_HALVES = {(8, 0), (10, 0), (12, 0), (15, 0)}
COPY_STEP = {6: 0, 12: 1}


def rope_angles(nc, const):
    pos = const.tile([P, MT], I32, name="pos")
    nc.gpsimd.iota(pos[:], pattern=[[P, MT]], base=0, channel_multiplier=1)
    ang = const.tile([P, 2, ROT, MT], F32, name="ang")

    def factor(j):
        return (1.0 / 1024.0) ** (j / 31.0)

    for j in range(4):
        nc.vector.tensor_scalar(out=ang[:, 0, j, :], in0=pos[:], scalar1=factor(j), scalar2=None, op0=ALU.mult)
    for j in (4, 8, 12):
        nc.vector.tensor_scalar(
            out=ang[:, 0, j : j + 4, :], in0=ang[:, 0, 0:4, :], scalar1=factor(j), scalar2=None, op0=ALU.mult
        )
    low = ang[:, 0, 0:16, :]
    nc.vector.tensor_scalar(out=ang[:, 0, 16:32, :], in0=low, scalar1=factor(16), scalar2=None, op0=ALU.mult)
    for j in (0, 16):
        nc.vector.tensor_scalar(
            out=ang[:, 1, j : j + 16, :], in0=low, scalar1=factor(j), scalar2=math.pi / 2.0, op0=ALU.mult, op1=ALU.add
        )
    ang_flat = ang[:].rearrange("p a j m -> p (a j m)")
    n = 2 * MT * ROT
    turns = const.tile([P, n], I32, name="turns")
    nc.vector.tensor_scalar(out=turns[:], in0=ang_flat, scalar1=1.0 / (2.0 * math.pi), scalar2=None, op0=ALU.mult)
    c1 = 6.28125
    c2 = 2.0 * math.pi - c1
    part = const.tile([P, n], F32, name="part")
    nc.vector.scalar_tensor_tensor(out=part[:], in0=turns[:], scalar=-c1, in1=ang_flat, op0=ALU.mult, op1=ALU.add)
    red = const.tile([P, n], F32, name="red")
    nc.vector.scalar_tensor_tensor(out=red[:], in0=turns[:], scalar=-c2, in1=part[:], op0=ALU.mult, op1=ALU.add)
    return red


def rope_tables(nc, const, red):
    cs = const.tile([P, MT, 2, 2, ROT], F32, name="cs")
    red4 = red[:].rearrange("p (a j m) -> p a m j", a=2, m=MT)
    nc.scalar.activation(out=cs[:, :, 0, 0, :], in_=red4[:, 1], func=ACT.Sin)
    nc.scalar.activation(out=cs[:, :, 0, 1, :], in_=red4[:, 1], func=ACT.Sin)
    nc.scalar.activation(out=cs[:, :, 1, 0, :], in_=red4[:, 0], func=ACT.Sin, scale=-1.0)
    nc.scalar.activation(out=cs[:, :, 1, 1, :], in_=red4[:, 0], func=ACT.Sin)
    return cs


def tile_groupedqueryattention_pa_kernel(tc, x, Wqkv_bytes, Wqkv_scale, out_0, out_1, out_2):
    nc = tc.nc
    w_view = Wqkv_bytes.rearrange("(g p t) n -> g p t n", p=P, t=PACK)
    x_view = x.rearrange("(m p) k -> p m k", p=P)
    out_q, out_k, out_v = (o.rearrange("l h d -> l (h d)") for o in (out_0, out_1, out_2))
    out_of = {"q": out_q, "k": out_k, "v": out_v}

    with ExitStack() as ctx:
        const = ctx.enter_context(tc.tile_pool(name="const", bufs=1))
        bytes_pool = ctx.enter_context(tc.tile_pool(name="bytes", bufs=1))
        xpool = ctx.enter_context(tc.tile_pool(name="xpool", bufs=1))
        shared = ctx.enter_context(tc.tile_pool(name="shared", bufs=1))
        wide_pool = ctx.enter_context(tc.tile_pool(name="wide", bufs=4))
        inter_pool = ctx.enter_context(tc.tile_pool(name="inter", bufs=3))
        code_pool = ctx.enter_context(tc.tile_pool(name="code", bufs=4))
        stage_pool = ctx.enter_context(tc.tile_pool(name="stage", bufs=4))
        tmp_pool = ctx.enter_context(tc.tile_pool(name="tmp", bufs=4))
        psum = ctx.enter_context(tc.psum_pool(name="psum", bufs=8))
        ctx.enter_context(tc.manual_schedule())

        zero = const.tile([P, 1], F32, name="zero")
        nc.vector.memset(zero[:], 0.0)
        junk = const.tile([P, 1], F32, name="junk")
        nc.scalar.activation(out=junk[:], in_=zero[:], func=ACT.Sin)

        wsc = const.tile([P, PASSES, PACK], F32, name="wsc")
        nc.sync.dma_start(out=wsc[:], in_=Wqkv_scale.rearrange("(g p t) o -> p g (t o)", p=P, t=PACK))

        wb = {}
        xraw = []

        def load_bytes(s):
            u, g = STEPS[s]
            c0, width = UNITS[u][1], UNITS[u][2]
            t_ = bytes_pool.tile([P, PACK, width], U8, name="wb%d" % s)
            nc.sync.dma_start(out=t_[:], in_=w_view[g][:, :, c0 : c0 + width])
            wb[s] = [t_[:, t, :] for t in range(PACK)]

        def load_plane(s, t):
            u, g = STEPS[s]
            c0, width = UNITS[u][1], UNITS[u][2]
            t_ = bytes_pool.tile([P, width], U8, name="wb%d_%d" % (s, t))
            nc.sync.dma_start(out=t_[:], in_=w_view[g][:, t, c0 : c0 + width])
            wb.setdefault(s, {})[t] = t_[:]

        def load_x(g):
            t_ = shared.tile([P, MT, 512], BF16, name="xraw%d" % g, offset=g * 4096)
            nc.sync.dma_start(out=t_[:], in_=x_view[:, :, g * 512 : (g + 1) * 512])
            xraw.append(t_)

        for s, t in HEAD_PLANES:
            load_plane(s, t)
        load_bytes(3)
        for g in range(PASSES):
            load_x(g)
        for s in range(4, N_STEPS):
            load_bytes(s)

        red = rope_angles(nc, const)

        ident = const.tile([P, P], F32, name="ident")
        make_identity(nc, ident[:])

        xc = xpool.tile([P, PASSES, 512], U32, name="xc", align_bytes=64)
        xs = xpool.tile([P, PASSES, 512], U8, name="xs", align_bytes=64)

        wide = {}
        inter = {}
        codes = {}
        banks = {}

        def widen_plane(s, t):
            u, g = STEPS[s]
            width = UNITS[u][2]
            if s not in wide:
                if width == 1024:
                    wt = wide_pool.tile([P, PACK, width], BF16, tag="wide")
                else:
                    wt = shared.tile([P, PACK, width], BF16, name="widekv%d" % s, offset=(s - 8) * 4096)
                wide[s] = wt
            wt = wide[s]
            src = wb[s][t].bitcast(FP8)
            if (s, t) in V_PLANES:
                nc.vector.tensor_scalar(out=wt[:, t, :], in0=src, scalar1=wsc[:, g, t : t + 1], scalar2=None, op0=ALU.mult)
            else:
                nc.scalar.activation(out=wt[:, t, :], in_=src, func=ACT.Copy, scale=wsc[:, g, t : t + 1])

        def widen(s):
            for t in range(PACK):
                widen_plane(s, t)

        def interleave(s):
            u, g = STEPS[s]
            kind, width = UNITS[u][0], UNITS[u][2]
            it = inter_pool.tile([P, PACK * width], BF16, tag="inter", align_bytes=64)
            inter[s] = it
            wt = wide[s]
            half = PACK * width // 2
            for q in range(2):
                dst = it[:, q * half : (q + 1) * half]
                if kind == "v":
                    dst = dst.rearrange("p (c i t) -> p c t i", i=RUN, t=PACK)
                    src = wt[:, :, q * width // 2 : (q + 1) * width // 2].rearrange("p t (c i) -> p c t i", i=RUN)
                else:
                    dst = dst.rearrange("p (hh c i t) -> p hh c t i", c=ROT // RUN, i=RUN, t=PACK)
                    src = wt[:].rearrange("p t (hh q c i) -> p q hh c t i", q=2, c=ROT // RUN, i=RUN)[:, q]
                if (s, q) in S_HALVES:
                    nc.scalar.copy(out=dst, in_=src)
                else:
                    nc.vector.tensor_copy(out=dst, in_=src)

        def quantize(s):
            width = UNITS[STEPS[s][0]][2]
            cd = code_pool.tile([P, width], U32, tag="codes", align_bytes=64)
            sc = code_pool.tile([P, width], U8, tag="scl", align_bytes=64)
            codes[s] = (cd, sc)
            nc.vector.quantize_mx(out=cd[:].bitcast(FP8X4), scales=sc[:], in_=inter[s][:])

        def multiply(s):
            u, g = STEPS[s]
            nb = UNITS[u][2] // 512
            if g == 0:
                for b in range(nb):
                    for m in range(MT):
                        bank = psum.tile([P, 512], F32, tag="bank")
                        banks[(u, m, b)] = bank
            cd, sc = codes[s]
            for m in range(MT):
                for b in range(nb):
                    nc.tensor.matmul_mx(
                        out=banks[(u, m, b)][:],
                        lhsT=xc[:, g, m * P : (m + 1) * P].bitcast(FP8X4),
                        lhsT_scale=xs[:, g, m * P : (m + 1) * P],
                        rhs=cd[:, b * 512 : (b + 1) * 512].bitcast(FP8X4),
                        rhs_scale=sc[:, b * 512 : (b + 1) * 512],
                        start=(g == 0),
                        stop=(g == PASSES - 1),
                    )

        stages = {}
        products = {}

        def stage(u, m):
            if (u, m) not in stages:
                kind, width = UNITS[u][0], UNITS[u][2]
                st = stage_pool.tile([P, width], F32, tag="stage_" + kind)
                stages[(u, m)] = st
            return stages[(u, m)]

        def copy_out(u, m):
            kind = UNITS[u][0]
            st = stage(u, m)
            if kind == "v":
                nc.scalar.copy(out=st[:], in_=banks[(u, m, 0)][:])
            else:
                src = banks[(u, m, 1)][:] if kind == "q" else banks[(u, m, 0)][:, 256:512]
                eng = nc.vector.tensor_copy if kind == "q" and m == MT - 1 else nc.scalar.copy
                eng(
                    out=st[:].rearrange("p (hh q j) -> p hh q j", q=2, j=ROT)[:, :, 1, :],
                    in_=src.rearrange("p (hh j) -> p hh j", j=ROT),
                )

        def rope_products(u, m):
            heads = UNITS[u][2] // 128
            src = banks[(u, m, 0)][:, 0 : heads * 2 * ROT]
            tmp = tmp_pool.tile([P, 2, heads, 2, ROT], F32, tag="tmp")
            products[(u, m)] = tmp
            nc.vector.tensor_tensor(
                out=tmp[:].rearrange("p a h f j -> p a h (f j)"),
                in0=src.rearrange("p (h fj) -> p h fj", fj=2 * ROT).unsqueeze(1).to_broadcast([P, 2, heads, 2 * ROT]),
                in1=cs[:, m].rearrange("p a f j -> p a (f j)").unsqueeze(2).to_broadcast([P, 2, heads, 2 * ROT]),
                op=ALU.mult,
            )

        def rope_sum(u, m):
            tmp = products[(u, m)]
            st5 = stage(u, m)[:].rearrange("p (h f q j) -> p h f q j", f=2, q=2, j=ROT)
            eng = nc.gpsimd if m < (3 if u < 2 else 2) else nc.vector
            eng.tensor_tensor(out=st5[:, :, :, 0, :], in0=tmp[:, 0], in1=tmp[:, 1][:, :, ::-1, :], op=ALU.add)

        def store(u, m):
            kind, c0, width = UNITS[u]
            c0 = c0 if kind == "q" else 0
            queue = nc.scalar if kind == "v" else nc.sync
            queue.dma_start(out=out_of[kind][m * P : (m + 1) * P, c0 : c0 + width], in_=stages[(u, m)][:])

        xg = []

        def x_turn(g):
            gt = shared.tile([P, MT * P * PACK], BF16, name="xg%d" % g, align_bytes=64, offset=(PASSES + g) * 4096)
            xg.append(gt)
            for h in range(2):
                xt = psum.tile([P, 4, P], F32, tag="bank")
                for mm in range(2):
                    words = xraw[g][:, 2 * h + mm, :].bitcast(F32)
                    for e in range(2):
                        nc.tensor.transpose(xt[:, 2 * mm + e, :], words[:, e : 256 : 2], ident[:])
                nc.scalar.copy(
                    out=gt[:, h * 1024 : (h + 1) * 1024].bitcast(F32).rearrange("p (mm r e) -> p mm r e", mm=2, e=2),
                    in_=xt[:].rearrange("p (mm e) r -> p mm r e", e=2),
                )

        def x_quant(g):
            nc.vector.quantize_mx(out=xc[:, g, :].bitcast(FP8X4), scales=xs[:, g, :], in_=xg[g][:])

        widen(0)
        widen(1)
        interleave(0)
        interleave(1)
        copied = set()
        rotated = set()
        waiting = []

        def banks_are_read(s):
            u, g = STEPS[s]
            if g > 0 or u == 0:
                return True
            if u == 1:
                return 0 in copied and 0 in rotated
            return 1 in (rotated if u == 2 else copied)

        for i in range(2, N_STEPS):
            widen(i)
            if i == 3:
                for g in range(PASSES):
                    x_turn(g)
                cs = rope_tables(nc, const, red)
            if i in COPY_STEP:
                u = COPY_STEP[i]
                for m in range(MT - 1):
                    copy_out(u, m)
                copied.add(u)
                if u in rotated:
                    for m in range(MT):
                        store(u, m)
            if i > 2:
                interleave(i - 1)
            if i in (6, 10):
                u = i // 4 - 1
                for m in range(MT):
                    rope_products(u, m)
                copy_out(u, MT - 1)
                rotated.add(u)
                for m in range(MT):
                    rope_sum(u, m)
                if u in copied:
                    for m in range(MT):
                        store(u, m)
            if i == 4:
                for g in range(PASSES):
                    x_quant(g)
            quantize(i - 2)
            waiting.append(i - 2)
            while i >= 4 and waiting and banks_are_read(waiting[0]):
                multiply(waiting.pop(0))

        interleave(15)
        quantize(14)
        multiply(14)
        for m in (0, 1):
            rope_products(2, m)
        for m in range(MT):
            copy_out(2, m)
        for m in (0, 1):
            rope_sum(2, m)
            store(2, m)
        quantize(15)
        multiply(15)
        for m in (2, 3):
            rope_products(2, m)
        for m in (2, 3):
            rope_sum(2, m)
            store(2, m)
        for m in range(MT):
            copy_out(3, m)
            if m > 0:
                store(3, m - 1)
        store(3, MT - 1)
